import numpy as np
import ml_dtypes


def mxq(x, axis, fmt="e4m3"):
    dtype, down = {"e4m3": (ml_dtypes.float8_e4m3fn, 7), "e5m2": (ml_dtypes.float8_e5m2, 14)}[fmt]
    v = np.moveaxis(np.asarray(x, np.float32).astype(ml_dtypes.bfloat16).astype(np.float64), axis, -1)
    blocks = v.reshape(v.shape[:-1] + (-1, 32))
    amax = np.abs(blocks).max(-1, keepdims=True)
    byte = np.maximum(np.where(amax > 0, np.frexp(amax)[1] - 1 + 127, 0) - down, 1)
    scale = np.exp2(byte - 127.0)
    codes = (blocks / scale).astype(np.float32).astype(dtype).astype(np.float64)
    return np.moveaxis((codes * scale).reshape(v.shape), -1, axis)


WIDE = False


def mx_kscale(k):
    if not WIDE:
        return np.ones(k)
    levels = np.array([10, -10, 5, -5, 0])
    a = np.random.permutation(np.resize(levels, k // 512 * 4)).reshape(k // 512, 4)
    idx = np.arange(k)
    return np.exp2(a[idx // 512, idx % 128 // 32])


BF16 = ml_dtypes.bfloat16


def bf(x):
    return np.asarray(x, np.float32).astype(BF16)


def f64(x):
    return np.asarray(x).astype(np.float64)


E2M1 = np.array([0.0, 0.5, 1.0, 1.5, 2.0, 3.0, 4.0, 6.0, -0.0, -0.5, -1.0, -1.5, -2.0, -3.0, -4.0, -6.0])


def pack_weight(w, fmt):
    k, n = w.shape
    w = f64(bf(w)).reshape(k // 32, 32, n)
    amax = np.abs(w).max(1)
    if fmt == "e4m3":
        byte = np.frexp(amax)[1] - 1 + 127 - 7
    else:
        mant, ex = np.frexp(amax / 6.0)
        byte = np.where(mant > 0.5, ex, ex - 1) + 127
    byte = np.clip(np.where(amax > 0, byte, 1), 1, 254)
    scaled = (w * np.exp2(127.0 - byte)[:, None, :]).reshape(k, n).astype(np.float32)
    by_word = np.ascontiguousarray(scaled.reshape(k // 512, 128, 4, n).transpose(0, 1, 3, 2))
    if fmt == "e4m3":
        words = by_word.astype(ml_dtypes.float8_e4m3fn).view(np.uint8)
    else:
        c = by_word.astype(ml_dtypes.float4_e2m1fn).view(np.uint8) & 0xF
        words = c[..., 0::2] | (c[..., 1::2] << 4)
    return np.ascontiguousarray(words), np.ascontiguousarray(byte.astype(np.uint8).reshape(k // 512, 16, n))


def unpack_weight(words, scales, fmt):
    g, p, n, _ = words.shape
    if fmt == "e4m3":
        vals = np.ascontiguousarray(words).view(ml_dtypes.float8_e4m3fn).astype(np.float64)
    else:
        nib = np.empty((g, p, n, 4), np.uint8)
        nib[..., 0::2] = words & 0xF
        nib[..., 1::2] = words >> 4
        vals = E2M1[nib]
    vals = vals * np.repeat(np.exp2(scales.astype(np.float64) - 127.0), 8, axis=1)[..., None]
    return vals.transpose(0, 1, 3, 2).reshape(g * 512, n)


B, T, DM, DH, L = 4, 2048, 512, 256, 512


def setup_inputs():
    s, u = mx_kscale(DM), mx_kscale(DM)
    k = bf(np.random.standard_normal((B, T, DM)) * s)
    v = bf(np.random.standard_normal((B, T, DM)) * u)
    Wk = np.random.standard_normal((DH, DM)) / np.sqrt(DM) / s
    Wv = np.random.standard_normal((DH, DM)) * 3.0 / np.sqrt(DM) / u
    Wk_words, Wk_scales = pack_weight(np.ascontiguousarray(Wk.T), "e4m3")
    Wv_words, Wv_scales = pack_weight(np.ascontiguousarray(Wv.T), "e4m3")
    return {"k": k,
            "v": v,
            "Wk_words": Wk_words, "Wk_scales": Wk_scales,
            "Wv_words": Wv_words, "Wv_scales": Wv_scales}


def reference(k, v, Wk_words, Wk_scales, Wv_words, Wv_scales):
    K = mxq(f64(k), 2, "e4m3") @ unpack_weight(Wk_words, Wk_scales, "e4m3")
    V = mxq(f64(v), 2, "e4m3") @ unpack_weight(Wv_words, Wv_scales, "e4m3")
    max_key = K.max(axis=0, keepdims=True)
    exp_key = np.exp(K - max_key)
    return exp_key * V, exp_key

@@ -1,0 +1,215 @@
+from contextlib import ExitStack
+
+import concourse.mybir as mybir
+from concourse.masks import make_identity
+
+F32 = mybir.dt.float32
+BF16 = mybir.dt.bfloat16
+I32 = mybir.dt.int32
+U32 = mybir.dt.uint32
+U8 = mybir.dt.uint8
+FP8X4 = mybir.dt.float8_e4m3fn_x4
+ALU = mybir.AluOpType
+EXP = mybir.ActivationFunctionType.Exp
+
+B, T, DM, DH = 4, 2048, 512, 256
+P = 128
+PACK = 4
+WORDS = DM // 2
+UNITS = T // P
+HALVES = DH // P
+LOAD_UNITS = 4
+CHUNKS = UNITS // LOAD_UNITS
+STORE_UNITS = 2
+PAIR = 2
+
+FLOPS = 2 * 2 * B * T * DM * DH
+
+
+def tile_aftfull_pa_t_kernel(tc, k, v, Wk_words, Wk_scales, Wv_words, Wv_scales, out_0, out_1):
+    nc = tc.nc
+    x_dram = {
+        "k": k.rearrange("b (p j) d -> p b j d", j=UNITS),
+        "v": v.rearrange("b (p j) d -> p b j d", j=UNITS),
+    }
+    w_dram = {"k": (Wk_words, Wk_scales), "v": (Wv_words, Wv_scales)}
+    weighted_dram = out_0.rearrange("b (p j) c -> p b j c", j=UNITS)
+    e_dram = out_1.rearrange("b (p j) c -> p b j c", j=UNITS)
+
+    with ExitStack() as stack:
+        const = stack.enter_context(tc.tile_pool(name="const", bufs=1))
+        x_pool = stack.enter_context(tc.tile_pool(name="x", bufs=2))
+        mx_pool = stack.enter_context(tc.tile_pool(name="mx", bufs=2))
+        max_pool = stack.enter_context(tc.tile_pool(name="max", bufs=4))
+        out_pool = stack.enter_context(tc.tile_pool(name="out", bufs=4))
+        xt_pool = stack.enter_context(tc.psum_pool(name="xt", bufs=4))
+        acc_pool = stack.enter_context(tc.psum_pool(name="acc", bufs=1))
+        stack.enter_context(tc.manual_schedule())
+
+        x_tiles = {}
+        xt_banks = {}
+        grouped = {}
+        packed = {}
+        w_codes = {}
+        w_plane = {}
+        acc = {}
+        e_tiles = {}
+        weighted_tiles = {}
+
+        def load(name, first, count):
+            chunk = first // LOAD_UNITS
+            if (name, chunk) not in x_tiles:
+                x_tiles[(name, chunk)] = x_pool.tile(
+                    [P, B, LOAD_UNITS, DM], BF16, name="x_" + name, tag="x_" + name
+                )
+            start = first % LOAD_UNITS
+            nc.sync.dma_start(
+                out=x_tiles[(name, chunk)][:, :, start : start + count, :],
+                in_=x_dram[name][:, :, first : first + count, :],
+            )
+
+        def load_weight(name):
+            words, scale_rows = w_dram[name]
+            w_codes[name] = const.tile([P, DH * PACK], U8, name="w_codes_" + name, align_bytes=64)
+            w_plane[name] = const.tile([P, DH], U8, name="w_plane_" + name, align_bytes=64)
+            nc.vector.memset(w_plane[name][:].bitcast(I32), 0)
+            nc.sync.dma_start(
+                out=w_codes[name][:].bitcast(I32),
+                in_=words[0].rearrange("p n t -> p (n t)").bitcast(I32),
+            )
+            for quadrant in range(4):
+                nc.sync.dma_start(
+                    out=w_plane[name][32 * quadrant : 32 * quadrant + 4, :].bitcast(I32),
+                    in_=scale_rows[0, 4 * quadrant : 4 * quadrant + 4, :].bitcast(I32),
+                )
+
+        def in_range(unit):
+            return 0 <= unit < UNITS
+
+        def transpose(name, unit):
+            if not in_range(unit):
+                return
+            x_tile = x_tiles[(name, unit // LOAD_UNITS)]
+            for pair in range(B // PAIR):
+                bank = xt_pool.tile([P, PAIR, 2, P], F32, name="xt")
+                xt_banks[(name, unit, pair)] = bank
+                for i in range(PAIR):
+                    row_words = x_tile[:, PAIR * pair + i, unit % LOAD_UNITS, :].bitcast(F32)
+                    for w in range(2):
+                        nc.tensor.transpose(bank[:, i, w, :], row_words[:, w:WORDS:2], identity[:])
+
+        def regroup(name, unit, pair):
+            if not in_range(unit):
+                return
+            if pair == 0:
+                grouped[(name, unit)] = mx_pool.tile(
+                    [P, B, P, PACK], BF16, name="grouped_" + name, tag="grouped_" + name, align_bytes=64
+                )
+            nc.scalar.copy(
+                out=grouped[(name, unit)][:, PAIR * pair : PAIR * (pair + 1), :, :].bitcast(F32),
+                in_=xt_banks[(name, unit, pair)][:].rearrange("p i w r -> p i r w"),
+            )
+
+        def quantise(name, unit):
+            if not in_range(unit):
+                return
+            codes = mx_pool.tile([P, B * P], U32, name="codes_" + name, tag="codes_" + name, align_bytes=64)
+            scales = mx_pool.tile([P, B * P], U8, name="scales_" + name, tag="scales_" + name, align_bytes=64)
+            packed[(name, unit)] = (codes, scales)
+            nc.vector.quantize_mx(
+                out=codes[:].bitcast(FP8X4),
+                scales=scales[:],
+                in_=grouped[(name, unit)][:].rearrange("p b r t -> p (b r t)"),
+            )
+
+        def project(name, unit):
+            if not in_range(unit):
+                return
+            codes, scales = packed[(name, unit)]
+            for half in range(HALVES):
+                bank = acc_pool.tile([P, B, P], F32, name="acc_%s%d" % (name, half), tag="acc_%s%d" % (name, half))
+                acc[(name, unit, half)] = bank
+                for b in range(B):
+                    nc.tensor.matmul_mx(
+                        out=bank[:, b, :],
+                        lhsT=codes[:, b * P : (b + 1) * P].bitcast(FP8X4),
+                        lhsT_scale=scales[:, b * P : (b + 1) * P],
+                        rhs=w_codes[name][:, half * P * PACK : (half + 1) * P * PACK].bitcast(FP8X4),
+                        rhs_scale=w_plane[name][:, half * P : (half + 1) * P],
+                        start=True,
+                        stop=True,
+                    )
+
+        def out_slice(tiles, unit, half):
+            return tiles[unit // STORE_UNITS][:, :, unit % STORE_UNITS, half * P : (half + 1) * P]
+
+        def soften(unit, half):
+            if not in_range(unit):
+                return
+            if unit % STORE_UNITS == 0 and half == 0:
+                e_tiles[unit // STORE_UNITS] = out_pool.tile([P, B, STORE_UNITS, DH], F32, name="e")
+            bank = acc[("k", unit, half)]
+            top = max_pool.tile([P, P], F32, name="top")
+            nc.vector.tensor_reduce(
+                out=top[:], in_=bank[:].rearrange("p b c -> p c b"), axis=mybir.AxisListType.X, op=ALU.max
+            )
+            e_part = out_slice(e_tiles, unit, half)
+            nc.vector.tensor_tensor(
+                out=e_part, in0=bank[:], in1=top[:].unsqueeze(1).to_broadcast([P, B, P]), op=ALU.subtract
+            )
+            nc.scalar.activation(out=e_part, in_=e_part, func=EXP)
+
+        def weigh(unit, half):
+            if not in_range(unit):
+                return
+            if unit % STORE_UNITS == 0 and half == 0:
+                weighted_tiles[unit // STORE_UNITS] = out_pool.tile([P, B, STORE_UNITS, DH], F32, name="weighted")
+            nc.vector.tensor_tensor(
+                out=out_slice(weighted_tiles, unit, half),
+                in0=acc[("v", unit, half)][:],
+                in1=out_slice(e_tiles, unit, half),
+                op=ALU.mult,
+            )
+
+        def store(dram, tiles, unit):
+            if not in_range(unit) or unit % STORE_UNITS != STORE_UNITS - 1:
+                return
+            group = unit // STORE_UNITS
+            nc.scalar.dma_start(
+                out=dram[:, :, group * STORE_UNITS : (group + 1) * STORE_UNITS, :], in_=tiles[group][:]
+            )
+
+        load("k", 0, 1)
+        load_weight("k")
+        load("v", 0, 1)
+        load_weight("v")
+        for unit in range(1, LOAD_UNITS):
+            load("k", unit, 1)
+            load("v", unit, 1)
+        for chunk in range(1, CHUNKS):
+            load("k", chunk * LOAD_UNITS, LOAD_UNITS)
+            load("v", chunk * LOAD_UNITS, LOAD_UNITS)
+
+        identity = const.tile([P, P], F32, name="identity")
+        make_identity(nc, identity[:])
+        warm = const.tile([P, 1], F32, name="warm")
+        nc.vector.memset(warm[:], 0.0)
+        nc.scalar.activation(out=warm[:], in_=warm[:], func=EXP)
+
+        for step in range(-2, UNITS + 1):
+            store(weighted_dram, weighted_tiles, step - 1)
+            quantise("k", step + 1)
+            project("v", step)
+            transpose("k", step + 2)
+            regroup("k", step + 2, 0)
+            soften(step, 0)
+            regroup("k", step + 2, 1)
+            soften(step, 1)
+            store(e_dram, e_tiles, step)
+            project("k", step + 1)
+            transpose("v", step + 2)
+            regroup("v", step + 2, 0)
+            regroup("v", step + 2, 1)
+            quantise("v", step + 1)
+            weigh(step, 0)
+            weigh(step, 1)

@@ -39,7 +39,7 @@ def tile_aftfull_pa_t_kernel(tc, k, v, Wk_words, Wk_scales, Wv_words, Wv_scales,
     with ExitStack() as stack:
         const = stack.enter_context(tc.tile_pool(name="const", bufs=1))
         x_pool = stack.enter_context(tc.tile_pool(name="x", bufs=2))
-        mx_pool = stack.enter_context(tc.tile_pool(name="mx", bufs=2))
+        mx_pool = stack.enter_context(tc.tile_pool(name="mx", bufs=3))
         max_pool = stack.enter_context(tc.tile_pool(name="max", bufs=4))
         out_pool = stack.enter_context(tc.tile_pool(name="out", bufs=4))
         xt_pool = stack.enter_context(tc.psum_pool(name="xt", bufs=4))
@@ -72,6 +72,7 @@ def tile_aftfull_pa_t_kernel(tc, k, v, Wk_words, Wk_scales, Wv_words, Wv_scales,
             words, scale_rows = w_dram[name]
             w_codes[name] = const.tile([P, DH * PACK], U8, name="w_codes_" + name, align_bytes=64)
             w_plane[name] = const.tile([P, DH], U8, name="w_plane_" + name, align_bytes=64)
+            landed = const.tile([P, 4, DH], U8, name="w_landed_" + name, align_bytes=64)
             nc.vector.memset(w_plane[name][:].bitcast(I32), 0)
             nc.sync.dma_start(
                 out=w_codes[name][:].bitcast(I32),
@@ -79,8 +80,13 @@ def tile_aftfull_pa_t_kernel(tc, k, v, Wk_words, Wk_scales, Wv_words, Wv_scales,
             )
             for quadrant in range(4):
                 nc.sync.dma_start(
-                    out=w_plane[name][32 * quadrant : 32 * quadrant + 4, :].bitcast(I32),
+                    out=landed[32 * quadrant : 32 * quadrant + 4, quadrant, :].bitcast(I32),
                     in_=scale_rows[0, 4 * quadrant : 4 * quadrant + 4, :].bitcast(I32),
+                )
+            for quadrant in range(4):
+                nc.vector.tensor_copy(
+                    out=w_plane[name][32 * quadrant : 32 * quadrant + 4, :].bitcast(I32),
+                    in_=landed[32 * quadrant : 32 * quadrant + 4, quadrant, :].bitcast(I32),
                 )
 
         def in_range(unit):
@@ -182,8 +188,10 @@ def tile_aftfull_pa_t_kernel(tc, k, v, Wk_words, Wk_scales, Wv_words, Wv_scales,
         load("k", 0, 1)
         load_weight("k")
         load("v", 0, 1)
+        load("k", 1, 1)
+        load("v", 1, 1)
         load_weight("v")
-        for unit in range(1, LOAD_UNITS):
+        for unit in range(2, LOAD_UNITS):
             load("k", unit, 1)
             load("v", unit, 1)
         for chunk in range(1, CHUNKS):
@@ -196,20 +204,20 @@ def tile_aftfull_pa_t_kernel(tc, k, v, Wk_words, Wk_scales, Wv_words, Wv_scales,
         nc.vector.memset(warm[:], 0.0)
         nc.scalar.activation(out=warm[:], in_=warm[:], func=EXP)
 
-        for step in range(-2, UNITS + 1):
-            store(weighted_dram, weighted_tiles, step - 1)
-            quantise("k", step + 1)
-            project("v", step)
-            transpose("k", step + 2)
+        for step in range(-3, UNITS + 1):
             regroup("k", step + 2, 0)
-            soften(step, 0)
             regroup("k", step + 2, 1)
+            regroup("v", step + 2, 0)
+            regroup("v", step + 2, 1)
+            soften(step, 0)
             soften(step, 1)
             store(e_dram, e_tiles, step)
             project("k", step + 1)
-            transpose("v", step + 2)
-            regroup("v", step + 2, 0)
-            regroup("v", step + 2, 1)
-            quantise("v", step + 1)
-            weigh(step, 0)
-            weigh(step, 1)
+            weigh(step - 1, 0)
+            weigh(step - 1, 1)
+            store(weighted_dram, weighted_tiles, step - 1)
+            project("v", step)
+            transpose("k", step + 3)
+            transpose("v", step + 3)
+            quantise("k", step + 2)
+            quantise("v", step + 2)

@@ -18,10 +18,12 @@ PACK = 4
 WORDS = DM // 2
 UNITS = T // P
 HALVES = DH // P
-LOAD_UNITS = 4
-CHUNKS = UNITS // LOAD_UNITS
-STORE_UNITS = 2
 PAIR = 2
+PAIRS = B // PAIR
+LOAD_UNITS = 4
+LOAD_AHEAD = 4
+STORE_UNITS = 2
+SIDE = {"k": 0, "v": 1}
 
 FLOPS = 2 * 2 * B * T * DM * DH
 
@@ -38,41 +40,46 @@ def tile_aftfull_pa_t_kernel(tc, k, v, Wk_words, Wk_scales, Wv_words, Wv_scales,
 
     with ExitStack() as stack:
         const = stack.enter_context(tc.tile_pool(name="const", bufs=1))
-        x_pool = stack.enter_context(tc.tile_pool(name="x", bufs=2))
+        x_unit_pool = stack.enter_context(tc.tile_pool(name="x_unit", bufs=LOAD_UNITS))
+        x_chunk_pool = stack.enter_context(tc.tile_pool(name="x_chunk", bufs=2))
         mx_pool = stack.enter_context(tc.tile_pool(name="mx", bufs=3))
-        max_pool = stack.enter_context(tc.tile_pool(name="max", bufs=4))
-        out_pool = stack.enter_context(tc.tile_pool(name="out", bufs=4))
+        work_pool = stack.enter_context(tc.tile_pool(name="work", bufs=3))
+        out_pool = stack.enter_context(tc.tile_pool(name="out", bufs=3))
         xt_pool = stack.enter_context(tc.psum_pool(name="xt", bufs=4))
         acc_pool = stack.enter_context(tc.psum_pool(name="acc", bufs=1))
         stack.enter_context(tc.manual_schedule())
 
-        x_tiles = {}
+        x_rows = {}
         xt_banks = {}
         grouped = {}
         packed = {}
         w_codes = {}
         w_plane = {}
-        acc = {}
+        k_banks = {}
+        v_banks = {}
+        diff = {}
         e_tiles = {}
         weighted_tiles = {}
 
+        def in_range(unit):
+            return 0 <= unit < UNITS
+
         def load(name, first, count):
-            chunk = first // LOAD_UNITS
-            if (name, chunk) not in x_tiles:
-                x_tiles[(name, chunk)] = x_pool.tile(
-                    [P, B, LOAD_UNITS, DM], BF16, name="x_" + name, tag="x_" + name
-                )
-            start = first % LOAD_UNITS
-            nc.sync.dma_start(
-                out=x_tiles[(name, chunk)][:, :, start : start + count, :],
-                in_=x_dram[name][:, :, first : first + count, :],
-            )
+            pool = x_unit_pool if count == 1 else x_chunk_pool
+            x_tile = pool.tile([P, B, count, DM], BF16, name="x_" + name, tag="x_" + name)
+            nc.sync.dma_start(out=x_tile[:], in_=x_dram[name][:, :, first : first + count, :])
+            for i in range(count):
+                x_rows[(name, first + i)] = x_tile[:, :, i, :]
+
+        def load_chunk_that_starts_with(unit):
+            if in_range(unit) and unit >= LOAD_UNITS and unit % LOAD_UNITS == 0:
+                load("k", unit, LOAD_UNITS)
+                load("v", unit, LOAD_UNITS)
 
         def load_weight(name):
             words, scale_rows = w_dram[name]
             w_codes[name] = const.tile([P, DH * PACK], U8, name="w_codes_" + name, align_bytes=64)
             w_plane[name] = const.tile([P, DH], U8, name="w_plane_" + name, align_bytes=64)
-            landed = const.tile([P, 4, DH], U8, name="w_landed_" + name, align_bytes=64)
             nc.vector.memset(w_plane[name][:].bitcast(I32), 0)
             nc.sync.dma_start(
                 out=w_codes[name][:].bitcast(I32),
@@ -80,111 +87,131 @@ def tile_aftfull_pa_t_kernel(tc, k, v, Wk_words, Wk_scales, Wv_words, Wv_scales,
             )
             for quadrant in range(4):
                 nc.sync.dma_start(
-                    out=landed[32 * quadrant : 32 * quadrant + 4, quadrant, :].bitcast(I32),
+                    out=w_plane[name][32 * quadrant : 32 * quadrant + 4, :].bitcast(I32),
                     in_=scale_rows[0, 4 * quadrant : 4 * quadrant + 4, :].bitcast(I32),
                 )
-            for quadrant in range(4):
-                nc.vector.tensor_copy(
-                    out=w_plane[name][32 * quadrant : 32 * quadrant + 4, :].bitcast(I32),
-                    in_=landed[32 * quadrant : 32 * quadrant + 4, quadrant, :].bitcast(I32),
-                )
-
-        def in_range(unit):
-            return 0 <= unit < UNITS
 
         def transpose(name, unit):
             if not in_range(unit):
                 return
-            x_tile = x_tiles[(name, unit // LOAD_UNITS)]
-            for pair in range(B // PAIR):
+            for pair in range(PAIRS):
                 bank = xt_pool.tile([P, PAIR, 2, P], F32, name="xt")
                 xt_banks[(name, unit, pair)] = bank
                 for i in range(PAIR):
-                    row_words = x_tile[:, PAIR * pair + i, unit % LOAD_UNITS, :].bitcast(F32)
+                    row_words = x_rows[(name, unit)][:, PAIR * pair + i, :].bitcast(F32)
                     for w in range(2):
                         nc.tensor.transpose(bank[:, i, w, :], row_words[:, w:WORDS:2], identity[:])
 
-        def regroup(name, unit, pair):
+        def regroup(name, unit):
             if not in_range(unit):
                 return
-            if pair == 0:
-                grouped[(name, unit)] = mx_pool.tile(
-                    [P, B, P, PACK], BF16, name="grouped_" + name, tag="grouped_" + name, align_bytes=64
+            if unit not in grouped:
+                grouped[unit] = mx_pool.tile([P, 2, B, P, PACK], BF16, name="grouped", align_bytes=64)
+            for pair in range(PAIRS):
+                nc.scalar.copy(
+                    out=grouped[unit][:, SIDE[name], PAIR * pair : PAIR * (pair + 1), :, :].bitcast(F32),
+                    in_=xt_banks[(name, unit, pair)][:].rearrange("p i w r -> p i r w"),
                 )
-            nc.scalar.copy(
-                out=grouped[(name, unit)][:, PAIR * pair : PAIR * (pair + 1), :, :].bitcast(F32),
-                in_=xt_banks[(name, unit, pair)][:].rearrange("p i w r -> p i r w"),
-            )
 
-        def quantise(name, unit):
+        def quantise(unit):
             if not in_range(unit):
                 return
-            codes = mx_pool.tile([P, B * P], U32, name="codes_" + name, tag="codes_" + name, align_bytes=64)
-            scales = mx_pool.tile([P, B * P], U8, name="scales_" + name, tag="scales_" + name, align_bytes=64)
-            packed[(name, unit)] = (codes, scales)
+            codes = mx_pool.tile([P, 2, B * P], U32, name="codes", align_bytes=64)
+            scales = mx_pool.tile([P, 2, B * P], U8, name="scales", align_bytes=64)
+            packed[unit] = (codes, scales)
             nc.vector.quantize_mx(
-                out=codes[:].bitcast(FP8X4),
-                scales=scales[:],
-                in_=grouped[(name, unit)][:].rearrange("p b r t -> p (b r t)"),
+                out=codes[:].rearrange("p s c -> p (s c)").bitcast(FP8X4),
+                scales=scales[:].rearrange("p s c -> p (s c)"),
+                in_=grouped[unit][:].rearrange("p s b r t -> p (s b r t)"),
             )
 
-        def project(name, unit):
+        def multiply(out, name, unit, b, first, count):
+            codes, scales = packed[unit]
+            nc.tensor.matmul_mx(
+                out=out,
+                lhsT=codes[:, SIDE[name], b * P : (b + 1) * P].bitcast(FP8X4),
+                lhsT_scale=scales[:, SIDE[name], b * P : (b + 1) * P],
+                rhs=w_codes[name][:, first * PACK : (first + count) * PACK].bitcast(FP8X4),
+                rhs_scale=w_plane[name][:, first : first + count],
+                start=True,
+                stop=True,
+            )
+
+        def project_k(unit):
             if not in_range(unit):
                 return
-            codes, scales = packed[(name, unit)]
             for half in range(HALVES):
-                bank = acc_pool.tile([P, B, P], F32, name="acc_%s%d" % (name, half), tag="acc_%s%d" % (name, half))
-                acc[(name, unit, half)] = bank
+                bank = acc_pool.tile([P, B, P], F32, name="k_bank%d" % half)
+                k_banks[(unit, half)] = bank
                 for b in range(B):
-                    nc.tensor.matmul_mx(
-                        out=bank[:, b, :],
-                        lhsT=codes[:, b * P : (b + 1) * P].bitcast(FP8X4),
-                        lhsT_scale=scales[:, b * P : (b + 1) * P],
-                        rhs=w_codes[name][:, half * P * PACK : (half + 1) * P * PACK].bitcast(FP8X4),
-                        rhs_scale=w_plane[name][:, half * P : (half + 1) * P],
-                        start=True,
-                        stop=True,
-                    )
+                    multiply(bank[:, b, :], "k", unit, b, half * P, P)
 
-        def out_slice(tiles, unit, half):
-            return tiles[unit // STORE_UNITS][:, :, unit % STORE_UNITS, half * P : (half + 1) * P]
-
-        def soften(unit, half):
+        def project_v(unit):
             if not in_range(unit):
                 return
-            if unit % STORE_UNITS == 0 and half == 0:
+            for pair in range(PAIRS):
+                bank = acc_pool.tile([P, PAIR, DH], F32, name="v_bank%d" % pair)
+                v_banks[(unit, pair)] = bank
+                for i in range(PAIR):
+                    multiply(bank[:, i, :], "v", unit, PAIR * pair + i, 0, DH)
+
+        def subtract_max(unit):
+            if not in_range(unit):
+                return
+            diff[unit] = work_pool.tile([P, HALVES, B, P], F32, name="diff")
+            for half in range(HALVES):
+                bank = k_banks[(unit, half)]
+                top = work_pool.tile([P, P], F32, name="top")
+                nc.vector.tensor_reduce(
+                    out=top[:], in_=bank[:].rearrange("p b c -> p c b"), axis=mybir.AxisListType.X, op=ALU.max
+                )
+                nc.vector.tensor_tensor(
+                    out=diff[unit][:, half, :, :],
+                    in0=bank[:],
+                    in1=top[:].unsqueeze(1).to_broadcast([P, B, P]),
+                    op=ALU.subtract,
+                )
+
+        def part(tiles, unit, pair):
+            return tiles[unit // STORE_UNITS][:, PAIR * pair : PAIR * (pair + 1), unit % STORE_UNITS, :]
+
+        def exponential(unit):
+            if not in_range(unit):
+                return
+            if unit % STORE_UNITS == 0:
                 e_tiles[unit // STORE_UNITS] = out_pool.tile([P, B, STORE_UNITS, DH], F32, name="e")
-            bank = acc[("k", unit, half)]
-            top = max_pool.tile([P, P], F32, name="top")
-            nc.vector.tensor_reduce(
-                out=top[:], in_=bank[:].rearrange("p b c -> p c b"), axis=mybir.AxisListType.X, op=ALU.max
+            nc.scalar.activation(
+                out=e_tiles[unit // STORE_UNITS][:, :, unit % STORE_UNITS, :].rearrange("p b (h c) -> p b h c", h=HALVES),
+                in_=diff[unit][:].rearrange("p h b c -> p b h c"),
+                func=EXP,
             )
-            e_part = out_slice(e_tiles, unit, half)
-            nc.vector.tensor_tensor(
-                out=e_part, in0=bank[:], in1=top[:].unsqueeze(1).to_broadcast([P, B, P]), op=ALU.subtract
-            )
-            nc.scalar.activation(out=e_part, in_=e_part, func=EXP)
 
-        def weigh(unit, half):
+        def weigh_on_gpsimd(unit):
             if not in_range(unit):
                 return
-            if unit % STORE_UNITS == 0 and half == 0:
+            if unit % STORE_UNITS == 0:
                 weighted_tiles[unit // STORE_UNITS] = out_pool.tile([P, B, STORE_UNITS, DH], F32, name="weighted")
+            v_copy = work_pool.tile([P, PAIR, DH], F32, name="v_copy")
+            nc.scalar.copy(out=v_copy[:], in_=v_banks[(unit, 1)][:])
+            nc.gpsimd.tensor_tensor(out=part(weighted_tiles, unit, 1), in0=v_copy[:], in1=part(e_tiles, unit, 1), op=ALU.mult)
+
+        def weigh_on_vector(unit):
+            if not in_range(unit):
+                return
             nc.vector.tensor_tensor(
-                out=out_slice(weighted_tiles, unit, half),
-                in0=acc[("v", unit, half)][:],
-                in1=out_slice(e_tiles, unit, half),
-                op=ALU.mult,
+                out=part(weighted_tiles, unit, 0), in0=v_banks[(unit, 0)][:], in1=part(e_tiles, unit, 0), op=ALU.mult
             )
 
         def store(dram, tiles, unit):
             if not in_range(unit) or unit % STORE_UNITS != STORE_UNITS - 1:
                 return
             group = unit // STORE_UNITS
-            nc.scalar.dma_start(
+            nc.sync.dma_start(
                 out=dram[:, :, group * STORE_UNITS : (group + 1) * STORE_UNITS, :], in_=tiles[group][:]
             )
 
+        identity = const.tile([P, P], F32, name="identity")
+        make_identity(nc, identity[:])
         load("k", 0, 1)
         load_weight("k")
         load("v", 0, 1)
@@ -194,30 +221,22 @@ def tile_aftfull_pa_t_kernel(tc, k, v, Wk_words, Wk_scales, Wv_words, Wv_scales,
         for unit in range(2, LOAD_UNITS):
             load("k", unit, 1)
             load("v", unit, 1)
-        for chunk in range(1, CHUNKS):
-            load("k", chunk * LOAD_UNITS, LOAD_UNITS)
-            load("v", chunk * LOAD_UNITS, LOAD_UNITS)
-
-        identity = const.tile([P, P], F32, name="identity")
-        make_identity(nc, identity[:])
         warm = const.tile([P, 1], F32, name="warm")
         nc.vector.memset(warm[:], 0.0)
         nc.scalar.activation(out=warm[:], in_=warm[:], func=EXP)
 
         for step in range(-3, UNITS + 1):
-            regroup("k", step + 2, 0)
-            regroup("k", step + 2, 1)
-            regroup("v", step + 2, 0)
-            regroup("v", step + 2, 1)
-            soften(step, 0)
-            soften(step, 1)
-            store(e_dram, e_tiles, step)
-            project("k", step + 1)
-            weigh(step - 1, 0)
-            weigh(step - 1, 1)
+            load_chunk_that_starts_with(step + 3 + LOAD_AHEAD)
+            weigh_on_gpsimd(step - 1)
+            regroup("k", step + 2)
+            regroup("v", step + 2)
+            subtract_max(step)
+            project_k(step + 1)
+            weigh_on_vector(step - 1)
             store(weighted_dram, weighted_tiles, step - 1)
-            project("v", step)
+            project_v(step)
+            exponential(step)
+            store(e_dram, e_tiles, step)
             transpose("k", step + 3)
             transpose("v", step + 3)
-            quantise("k", step + 2)
-            quantise("v", step + 2)
+            quantise(step + 2)

@@ -20,9 +20,7 @@ UNITS = T // P
 HALVES = DH // P
 PAIR = 2
 PAIRS = B // PAIR
-LOAD_UNITS = 4
-LOAD_AHEAD = 4
-STORE_UNITS = 2
+MAX_PIECE = 4
 SIDE = {"k": 0, "v": 1}
 
 FLOPS = 2 * 2 * B * T * DM * DH
@@ -40,11 +38,10 @@ def tile_aftfull_pa_t_kernel(tc, k, v, Wk_words, Wk_scales, Wv_words, Wv_scales,
 
     with ExitStack() as stack:
         const = stack.enter_context(tc.tile_pool(name="const", bufs=1))
-        x_unit_pool = stack.enter_context(tc.tile_pool(name="x_unit", bufs=LOAD_UNITS))
-        x_chunk_pool = stack.enter_context(tc.tile_pool(name="x_chunk", bufs=2))
+        x_pool = stack.enter_context(tc.tile_pool(name="x", bufs=3))
         mx_pool = stack.enter_context(tc.tile_pool(name="mx", bufs=3))
         work_pool = stack.enter_context(tc.tile_pool(name="work", bufs=3))
-        out_pool = stack.enter_context(tc.tile_pool(name="out", bufs=3))
+        out_pool = stack.enter_context(tc.tile_pool(name="out", bufs=2))
         xt_pool = stack.enter_context(tc.psum_pool(name="xt", bufs=4))
         acc_pool = stack.enter_context(tc.psum_pool(name="acc", bufs=1))
         stack.enter_context(tc.manual_schedule())
@@ -61,20 +58,24 @@ def tile_aftfull_pa_t_kernel(tc, k, v, Wk_words, Wk_scales, Wv_words, Wv_scales,
         e_tiles = {}
         weighted_tiles = {}
 
+        sizes = []
+        while sum(sizes) < UNITS:
+            sizes.append(min(MAX_PIECE, max(1, sum(sizes))))
+        loads = [(sum(sizes[:i]), sizes[i]) for i in range(len(sizes))]
+        stores = [(UNITS - first - count, count) for first, count in reversed(loads)]
+        store_of = {}
+        for first, count in stores:
+            for unit in range(first, first + count):
+                store_of[unit] = (first, count)
+
         def in_range(unit):
             return 0 <= unit < UNITS
 
         def load(name, first, count):
-            pool = x_unit_pool if count == 1 else x_chunk_pool
-            x_tile = pool.tile([P, B, count, DM], BF16, name="x_" + name, tag="x_" + name)
+            x_tile = x_pool.tile([P, B, count, DM], BF16, name="x_" + name, tag="x_" + name)
             nc.sync.dma_start(out=x_tile[:], in_=x_dram[name][:, :, first : first + count, :])
             for i in range(count):
                 x_rows[(name, first + i)] = x_tile[:, :, i, :]
-
-        def load_chunk_that_starts_with(unit):
-            if in_range(unit) and unit >= LOAD_UNITS and unit % LOAD_UNITS == 0:
-                load("k", unit, LOAD_UNITS)
-                load("v", unit, LOAD_UNITS)
 
         def load_weight(name):
             words, scale_rows = w_dram[name]
@@ -172,16 +173,17 @@ def tile_aftfull_pa_t_kernel(tc, k, v, Wk_words, Wk_scales, Wv_words, Wv_scales,
                     op=ALU.subtract,
                 )
 
-        def part(tiles, unit, pair):
-            return tiles[unit // STORE_UNITS][:, PAIR * pair : PAIR * (pair + 1), unit % STORE_UNITS, :]
+        def output_tile(tiles, name, unit):
+            first, count = store_of[unit]
+            if unit == first:
+                tiles[first] = out_pool.tile([P, B, count, DH], F32, name=name, tag=name)
+            return tiles[first][:, :, unit - first, :]
 
         def exponential(unit):
             if not in_range(unit):
                 return
-            if unit % STORE_UNITS == 0:
-                e_tiles[unit // STORE_UNITS] = out_pool.tile([P, B, STORE_UNITS, DH], F32, name="e")
             nc.scalar.activation(
-                out=e_tiles[unit // STORE_UNITS][:, :, unit % STORE_UNITS, :].rearrange("p b (h c) -> p b h c", h=HALVES),
+                out=output_tile(e_tiles, "e", unit).rearrange("p b (h c) -> p b h c", h=HALVES),
                 in_=diff[unit][:].rearrange("p h b c -> p b h c"),
                 func=EXP,
             )
@@ -189,44 +191,45 @@ def tile_aftfull_pa_t_kernel(tc, k, v, Wk_words, Wk_scales, Wv_words, Wv_scales,
         def weigh_on_gpsimd(unit):
             if not in_range(unit):
                 return
-            if unit % STORE_UNITS == 0:
-                weighted_tiles[unit // STORE_UNITS] = out_pool.tile([P, B, STORE_UNITS, DH], F32, name="weighted")
             v_copy = work_pool.tile([P, PAIR, DH], F32, name="v_copy")
             nc.scalar.copy(out=v_copy[:], in_=v_banks[(unit, 1)][:])
-            nc.gpsimd.tensor_tensor(out=part(weighted_tiles, unit, 1), in0=v_copy[:], in1=part(e_tiles, unit, 1), op=ALU.mult)
+            nc.gpsimd.tensor_tensor(
+                out=output_tile(weighted_tiles, "weighted", unit)[:, PAIR:B, :],
+                in0=v_copy[:],
+                in1=e_tiles[store_of[unit][0]][:, PAIR:B, unit - store_of[unit][0], :],
+                op=ALU.mult,
+            )
 
         def weigh_on_vector(unit):
             if not in_range(unit):
                 return
+            first = store_of[unit][0]
             nc.vector.tensor_tensor(
-                out=part(weighted_tiles, unit, 0), in0=v_banks[(unit, 0)][:], in1=part(e_tiles, unit, 0), op=ALU.mult
+                out=weighted_tiles[first][:, 0:PAIR, unit - first, :],
+                in0=v_banks[(unit, 0)][:],
+                in1=e_tiles[first][:, 0:PAIR, unit - first, :],
+                op=ALU.mult,
             )
 
         def store(dram, tiles, unit):
-            if not in_range(unit) or unit % STORE_UNITS != STORE_UNITS - 1:
+            if not in_range(unit):
                 return
-            group = unit // STORE_UNITS
-            nc.sync.dma_start(
-                out=dram[:, :, group * STORE_UNITS : (group + 1) * STORE_UNITS, :], in_=tiles[group][:]
-            )
+            first, count = store_of[unit]
+            if unit == first + count - 1:
+                nc.sync.dma_start(out=dram[:, :, first : first + count, :], in_=tiles[first][:])
 
         identity = const.tile([P, P], F32, name="identity")
         make_identity(nc, identity[:])
-        load("k", 0, 1)
-        load_weight("k")
-        load("v", 0, 1)
-        load("k", 1, 1)
-        load("v", 1, 1)
-        load_weight("v")
-        for unit in range(2, LOAD_UNITS):
-            load("k", unit, 1)
-            load("v", unit, 1)
+        for i, (first, count) in enumerate(loads):
+            load("k", first, count)
+            load("v", first, count)
+            if i < 2:
+                load_weight(("k", "v")[i])
         warm = const.tile([P, 1], F32, name="warm")
         nc.vector.memset(warm[:], 0.0)
         nc.scalar.activation(out=warm[:], in_=warm[:], func=EXP)
 
         for step in range(-3, UNITS + 1):
-            load_chunk_that_starts_with(step + 3 + LOAD_AHEAD)
             weigh_on_gpsimd(step - 1)
             regroup("k", step + 2)
             regroup("v", step + 2)

@@ -38,7 +38,8 @@ def tile_aftfull_pa_t_kernel(tc, k, v, Wk_words, Wk_scales, Wv_words, Wv_scales,
 
     with ExitStack() as stack:
         const = stack.enter_context(tc.tile_pool(name="const", bufs=1))
-        x_pool = stack.enter_context(tc.tile_pool(name="x", bufs=3))
+        x_unit_pool = stack.enter_context(tc.tile_pool(name="x_unit", bufs=MAX_PIECE))
+        x_chunk_pool = stack.enter_context(tc.tile_pool(name="x_chunk", bufs=2))
         mx_pool = stack.enter_context(tc.tile_pool(name="mx", bufs=3))
         work_pool = stack.enter_context(tc.tile_pool(name="work", bufs=3))
         out_pool = stack.enter_context(tc.tile_pool(name="out", bufs=2))
@@ -58,11 +59,12 @@ def tile_aftfull_pa_t_kernel(tc, k, v, Wk_words, Wk_scales, Wv_words, Wv_scales,
         e_tiles = {}
         weighted_tiles = {}
 
-        sizes = []
-        while sum(sizes) < UNITS:
-            sizes.append(min(MAX_PIECE, max(1, sum(sizes))))
-        loads = [(sum(sizes[:i]), sizes[i]) for i in range(len(sizes))]
-        stores = [(UNITS - first - count, count) for first, count in reversed(loads)]
+        loads = [(unit, 1) for unit in range(MAX_PIECE)]
+        loads.extend((first, MAX_PIECE) for first in range(MAX_PIECE, UNITS, MAX_PIECE))
+        stores = []
+        while sum(count for first, count in stores) < UNITS:
+            left = UNITS - sum(count for first, count in stores)
+            stores.append((UNITS - left, min(MAX_PIECE, max(1, left // 2))))
         store_of = {}
         for first, count in stores:
             for unit in range(first, first + count):
@@ -72,7 +74,8 @@ def tile_aftfull_pa_t_kernel(tc, k, v, Wk_words, Wk_scales, Wv_words, Wv_scales,
             return 0 <= unit < UNITS
 
         def load(name, first, count):
-            x_tile = x_pool.tile([P, B, count, DM], BF16, name="x_" + name, tag="x_" + name)
+            pool = x_unit_pool if count == 1 else x_chunk_pool
+            x_tile = pool.tile([P, B, count, DM], BF16, name="x_" + name, tag="x_" + name)
             nc.sync.dma_start(out=x_tile[:], in_=x_dram[name][:, :, first : first + count, :])
             for i in range(count):
                 x_rows[(name, first + i)] = x_tile[:, :, i, :]
@@ -160,16 +163,19 @@ def tile_aftfull_pa_t_kernel(tc, k, v, Wk_words, Wk_scales, Wv_words, Wv_scales,
             if not in_range(unit):
                 return
             diff[unit] = work_pool.tile([P, HALVES, B, P], F32, name="diff")
+            top = work_pool.tile([P, HALVES, P], F32, name="top")
             for half in range(HALVES):
-                bank = k_banks[(unit, half)]
-                top = work_pool.tile([P, P], F32, name="top")
                 nc.vector.tensor_reduce(
-                    out=top[:], in_=bank[:].rearrange("p b c -> p c b"), axis=mybir.AxisListType.X, op=ALU.max
+                    out=top[:, half, :],
+                    in_=k_banks[(unit, half)][:].rearrange("p b c -> p c b"),
+                    axis=mybir.AxisListType.X,
+                    op=ALU.max,
                 )
+            for half in range(HALVES):
                 nc.vector.tensor_tensor(
                     out=diff[unit][:, half, :, :],
-                    in0=bank[:],
-                    in1=top[:].unsqueeze(1).to_broadcast([P, B, P]),
+                    in0=k_banks[(unit, half)][:],
+                    in1=top[:, half, :].unsqueeze(1).to_broadcast([P, B, P]),
                     op=ALU.subtract,
                 )
 

@@ -21,6 +21,7 @@ HALVES = DH // P
 PAIR = 2
 PAIRS = B // PAIR
 MAX_PIECE = 4
+STORE_PIECE = 2
 SIDE = {"k": 0, "v": 1}
 
 FLOPS = 2 * 2 * B * T * DM * DH
@@ -42,7 +43,7 @@ def tile_aftfull_pa_t_kernel(tc, k, v, Wk_words, Wk_scales, Wv_words, Wv_scales,
         x_chunk_pool = stack.enter_context(tc.tile_pool(name="x_chunk", bufs=2))
         mx_pool = stack.enter_context(tc.tile_pool(name="mx", bufs=3))
         work_pool = stack.enter_context(tc.tile_pool(name="work", bufs=3))
-        out_pool = stack.enter_context(tc.tile_pool(name="out", bufs=2))
+        out_pool = stack.enter_context(tc.tile_pool(name="out", bufs=4))
         xt_pool = stack.enter_context(tc.psum_pool(name="xt", bufs=4))
         acc_pool = stack.enter_context(tc.psum_pool(name="acc", bufs=1))
         stack.enter_context(tc.manual_schedule())
@@ -60,11 +61,12 @@ def tile_aftfull_pa_t_kernel(tc, k, v, Wk_words, Wk_scales, Wv_words, Wv_scales,
         weighted_tiles = {}
 
         loads = [(unit, 1) for unit in range(MAX_PIECE)]
-        loads.extend((first, MAX_PIECE) for first in range(MAX_PIECE, UNITS, MAX_PIECE))
+        loads.extend((first, MAX_PIECE) for first in range(MAX_PIECE, UNITS - MAX_PIECE, MAX_PIECE))
+        loads.extend((unit, 1) for unit in range(UNITS - MAX_PIECE, UNITS))
         stores = []
         while sum(count for first, count in stores) < UNITS:
             left = UNITS - sum(count for first, count in stores)
-            stores.append((UNITS - left, min(MAX_PIECE, max(1, left // 2))))
+            stores.append((UNITS - left, min(STORE_PIECE, max(1, left // 2))))
         store_of = {}
         for first, count in stores:
             for unit in range(first, first + count):

@@ -17,7 +17,6 @@ P = 128
 PACK = 4
 WORDS = DM // 2
 UNITS = T // P
-HALVES = DH // P
 PAIR = 2
 PAIRS = B // PAIR
 MAX_PIECE = 4
@@ -56,6 +55,9 @@ def tile_aftfull_pa_t_kernel(tc, k, v, Wk_words, Wk_scales, Wv_words, Wv_scales,
         w_plane = {}
         k_banks = {}
         v_banks = {}
+        k_high = {}
+        pair_top = {}
+        top = {}
         diff = {}
         e_tiles = {}
         weighted_tiles = {}
@@ -143,79 +145,76 @@ def tile_aftfull_pa_t_kernel(tc, k, v, Wk_words, Wk_scales, Wv_words, Wv_scales,
                 stop=True,
             )
 
-        def project_k(unit):
+        def project(banks, name, unit, pair):
             if not in_range(unit):
                 return
-            for half in range(HALVES):
-                bank = acc_pool.tile([P, B, P], F32, name="k_bank%d" % half)
-                k_banks[(unit, half)] = bank
-                for b in range(B):
-                    multiply(bank[:, b, :], "k", unit, b, half * P, P)
+            bank = acc_pool.tile([P, PAIR, DH], F32, name="%s_bank%d" % (name, pair))
+            banks[(unit, pair)] = bank
+            for i in range(PAIR):
+                multiply(bank[:, i, :], name, unit, PAIR * pair + i, 0, DH)
 
-        def project_v(unit):
+        def copy_k_high(unit):
             if not in_range(unit):
                 return
-            for pair in range(PAIRS):
-                bank = acc_pool.tile([P, PAIR, DH], F32, name="v_bank%d" % pair)
-                v_banks[(unit, pair)] = bank
-                for i in range(PAIR):
-                    multiply(bank[:, i, :], "v", unit, PAIR * pair + i, 0, DH)
+            k_high[unit] = work_pool.tile([P, PAIR, DH], F32, name="k_high")
+            nc.scalar.copy(out=k_high[unit][:], in_=k_banks[(unit, 1)][:])
 
-        def subtract_max(unit):
+        def max_of_pairs(unit):
             if not in_range(unit):
                 return
-            diff[unit] = work_pool.tile([P, HALVES, B, P], F32, name="diff")
-            top = work_pool.tile([P, HALVES, P], F32, name="top")
-            for half in range(HALVES):
-                nc.vector.tensor_reduce(
-                    out=top[:, half, :],
-                    in_=k_banks[(unit, half)][:].rearrange("p b c -> p c b"),
-                    axis=mybir.AxisListType.X,
-                    op=ALU.max,
-                )
-            for half in range(HALVES):
-                nc.vector.tensor_tensor(
-                    out=diff[unit][:, half, :, :],
-                    in0=k_banks[(unit, half)][:],
-                    in1=top[:, half, :].unsqueeze(1).to_broadcast([P, B, P]),
-                    op=ALU.subtract,
-                )
+            pair_top[unit] = work_pool.tile([P, PAIR, DH], F32, name="pair_top")
+            nc.vector.tensor_tensor(
+                out=pair_top[unit][:], in0=k_banks[(unit, 0)][:], in1=k_high[unit][:], op=ALU.max
+            )
+
+        def max_of_batch(unit):
+            if not in_range(unit):
+                return
+            top[unit] = work_pool.tile([P, DH], F32, name="top")
+            nc.vector.tensor_tensor(
+                out=top[unit][:], in0=pair_top[unit][:, 0, :], in1=pair_top[unit][:, 1, :], op=ALU.max
+            )
+            diff[unit] = work_pool.tile([P, B, DH], F32, name="diff")
+
+        def subtract_high(unit):
+            if not in_range(unit):
+                return
+            nc.gpsimd.tensor_tensor(
+                out=diff[unit][:, PAIR:B, :],
+                in0=k_high[unit][:],
+                in1=top[unit][:].unsqueeze(1).to_broadcast([P, PAIR, DH]),
+                op=ALU.subtract,
+            )
+
+        def subtract_low(unit):
+            if not in_range(unit):
+                return
+            nc.vector.tensor_tensor(
+                out=diff[unit][:, 0:PAIR, :],
+                in0=k_banks[(unit, 0)][:],
+                in1=top[unit][:].unsqueeze(1).to_broadcast([P, PAIR, DH]),
+                op=ALU.subtract,
+            )
 
         def output_tile(tiles, name, unit):
             first, count = store_of[unit]
-            if unit == first:
+            if unit == first and first not in tiles:
                 tiles[first] = out_pool.tile([P, B, count, DH], F32, name=name, tag=name)
             return tiles[first][:, :, unit - first, :]
 
         def exponential(unit):
             if not in_range(unit):
                 return
-            nc.scalar.activation(
-                out=output_tile(e_tiles, "e", unit).rearrange("p b (h c) -> p b h c", h=HALVES),
-                in_=diff[unit][:].rearrange("p h b c -> p b h c"),
-                func=EXP,
-            )
+            nc.scalar.activation(out=output_tile(e_tiles, "e", unit), in_=diff[unit][:], func=EXP)
 
-        def weigh_on_gpsimd(unit):
+        def weigh(unit, pair):
             if not in_range(unit):
                 return
-            v_copy = work_pool.tile([P, PAIR, DH], F32, name="v_copy")
-            nc.scalar.copy(out=v_copy[:], in_=v_banks[(unit, 1)][:])
-            nc.gpsimd.tensor_tensor(
-                out=output_tile(weighted_tiles, "weighted", unit)[:, PAIR:B, :],
-                in0=v_copy[:],
-                in1=e_tiles[store_of[unit][0]][:, PAIR:B, unit - store_of[unit][0], :],
-                op=ALU.mult,
-            )
-
-        def weigh_on_vector(unit):
-            if not in_range(unit):
-                return
-            first = store_of[unit][0]
+            items = slice(PAIR * pair, PAIR * (pair + 1))
             nc.vector.tensor_tensor(
-                out=weighted_tiles[first][:, 0:PAIR, unit - first, :],
-                in0=v_banks[(unit, 0)][:],
-                in1=e_tiles[first][:, 0:PAIR, unit - first, :],
+                out=output_tile(weighted_tiles, "weighted", unit)[:, items, :],
+                in0=v_banks[(unit, pair)][:],
+                in1=output_tile(e_tiles, "e", unit)[:, items, :],
                 op=ALU.mult,
             )
 
@@ -238,14 +237,20 @@ def tile_aftfull_pa_t_kernel(tc, k, v, Wk_words, Wk_scales, Wv_words, Wv_scales,
         nc.scalar.activation(out=warm[:], in_=warm[:], func=EXP)
 
         for step in range(-3, UNITS + 1):
-            weigh_on_gpsimd(step - 1)
             regroup("k", step + 2)
             regroup("v", step + 2)
-            subtract_max(step)
-            project_k(step + 1)
-            weigh_on_vector(step - 1)
+            project(k_banks, "k", step + 1, 1)
+            copy_k_high(step + 1)
+            max_of_pairs(step)
+            weigh(step - 1, 0)
+            project(v_banks, "v", step, 0)
+            max_of_batch(step)
+            subtract_high(step)
+            weigh(step - 1, 1)
             store(weighted_dram, weighted_tiles, step - 1)
-            project_v(step)
+            project(v_banks, "v", step, 1)
+            subtract_low(step)
+            project(k_banks, "k", step + 1, 0)
             exponential(step)
             store(e_dram, e_tiles, step)
             transpose("k", step + 3)

@@ -19,9 +19,10 @@ WORDS = DM // 2
 UNITS = T // P
 PAIR = 2
 PAIRS = B // PAIR
-MAX_PIECE = 4
-STORE_PIECE = 2
+GROUP = 4
+LOAD_PIECES = (1, 2, 4, 4)
 SIDE = {"k": 0, "v": 1}
+IO_TAG = {"k": "k_e", "e": "k_e", "v": "v_w", "weighted": "v_w"}
 
 FLOPS = 2 * 2 * B * T * DM * DH
 
@@ -38,11 +39,9 @@ def tile_aftfull_pa_t_kernel(tc, k, v, Wk_words, Wk_scales, Wv_words, Wv_scales,
 
     with ExitStack() as stack:
         const = stack.enter_context(tc.tile_pool(name="const", bufs=1))
-        x_unit_pool = stack.enter_context(tc.tile_pool(name="x_unit", bufs=MAX_PIECE))
-        x_chunk_pool = stack.enter_context(tc.tile_pool(name="x_chunk", bufs=2))
+        io_pool = stack.enter_context(tc.tile_pool(name="io", bufs=UNITS // GROUP + 1))
         mx_pool = stack.enter_context(tc.tile_pool(name="mx", bufs=3))
         work_pool = stack.enter_context(tc.tile_pool(name="work", bufs=3))
-        out_pool = stack.enter_context(tc.tile_pool(name="out", bufs=4))
         xt_pool = stack.enter_context(tc.psum_pool(name="xt", bufs=4))
         acc_pool = stack.enter_context(tc.psum_pool(name="acc", bufs=1))
         stack.enter_context(tc.manual_schedule())
@@ -62,13 +61,10 @@ def tile_aftfull_pa_t_kernel(tc, k, v, Wk_words, Wk_scales, Wv_words, Wv_scales,
         e_tiles = {}
         weighted_tiles = {}
 
-        loads = [(unit, 1) for unit in range(MAX_PIECE)]
-        loads.extend((first, MAX_PIECE) for first in range(MAX_PIECE, UNITS - MAX_PIECE, MAX_PIECE))
-        loads.extend((unit, 1) for unit in range(UNITS - MAX_PIECE, UNITS))
         stores = []
         while sum(count for first, count in stores) < UNITS:
             left = UNITS - sum(count for first, count in stores)
-            stores.append((UNITS - left, min(STORE_PIECE, max(1, left // 2))))
+            stores.append((UNITS - left, min(GROUP, max(1, left // 2))))
         store_of = {}
         for first, count in stores:
             for unit in range(first, first + count):
@@ -77,12 +73,11 @@ def tile_aftfull_pa_t_kernel(tc, k, v, Wk_words, Wk_scales, Wv_words, Wv_scales,
         def in_range(unit):
             return 0 <= unit < UNITS
 
-        def load(name, first, count):
-            pool = x_unit_pool if count == 1 else x_chunk_pool
-            x_tile = pool.tile([P, B, count, DM], BF16, name="x_" + name, tag="x_" + name)
-            nc.sync.dma_start(out=x_tile[:], in_=x_dram[name][:, :, first : first + count, :])
+        def load(name, tile_of_group, first, count):
+            piece = (first % GROUP) // count
+            nc.sync.dma_start(out=tile_of_group[:, piece, :, :, :], in_=x_dram[name][:, :, first : first + count, :])
             for i in range(count):
-                x_rows[(name, first + i)] = x_tile[:, :, i, :]
+                x_rows[(name, first + i)] = tile_of_group[:, piece, :, i, :]
 
         def load_weight(name):
             words, scale_rows = w_dram[name]
@@ -199,7 +194,7 @@ def tile_aftfull_pa_t_kernel(tc, k, v, Wk_words, Wk_scales, Wv_words, Wv_scales,
         def output_tile(tiles, name, unit):
             first, count = store_of[unit]
             if unit == first and first not in tiles:
-                tiles[first] = out_pool.tile([P, B, count, DH], F32, name=name, tag=name)
+                tiles[first] = io_pool.tile([P, B, count, DH], F32, name=name, tag=IO_TAG[name])
             return tiles[first][:, :, unit - first, :]
 
         def exponential(unit):
@@ -227,11 +222,19 @@ def tile_aftfull_pa_t_kernel(tc, k, v, Wk_words, Wk_scales, Wv_words, Wv_scales,
 
         identity = const.tile([P, P], F32, name="identity")
         make_identity(nc, identity[:])
-        for i, (first, count) in enumerate(loads):
-            load("k", first, count)
-            load("v", first, count)
-            if i < 2:
-                load_weight(("k", "v")[i])
+        weights_left = ["k", "v"]
+        for group, count in enumerate(LOAD_PIECES):
+            x_tiles = {}
+            for name in ("k", "v"):
+                x_tiles[name] = io_pool.tile(
+                    [P, GROUP // count, B, count, DM], BF16, name="x_" + name, tag=IO_TAG[name]
+                )
+            for first in range(group * GROUP, (group + 1) * GROUP, count):
+                load("k", x_tiles["k"], first, count)
+                load("v", x_tiles["v"], first, count)
+                if weights_left:
+                    load_weight(weights_left[0])
+                    weights_left.remove(weights_left[0])
         warm = const.tile([P, 1], F32, name="warm")
         nc.vector.memset(warm[:], 0.0)
         nc.scalar.activation(out=warm[:], in_=warm[:], func=EXP)

@@ -108,32 +108,31 @@ def tile_aftfull_pa_t_kernel(tc, k, v, Wk_words, Wk_scales, Wv_words, Wv_scales,
         def regroup(name, unit):
             if not in_range(unit):
                 return
-            if unit not in grouped:
-                grouped[unit] = mx_pool.tile([P, 2, B, P, PACK], BF16, name="grouped", align_bytes=64)
+            grouped[(name, unit)] = mx_pool.tile([P, B, P, PACK], BF16, name="grouped_" + name, align_bytes=64)
             for pair in range(PAIRS):
                 nc.scalar.copy(
-                    out=grouped[unit][:, SIDE[name], PAIR * pair : PAIR * (pair + 1), :, :].bitcast(F32),
+                    out=grouped[(name, unit)][:, PAIR * pair : PAIR * (pair + 1), :, :].bitcast(F32),
                     in_=xt_banks[(name, unit, pair)][:].rearrange("p i w r -> p i r w"),
                 )
 
-        def quantise(unit):
+        def quantise(name, unit):
             if not in_range(unit):
                 return
-            codes = mx_pool.tile([P, 2, B * P], U32, name="codes", align_bytes=64)
-            scales = mx_pool.tile([P, 2, B * P], U8, name="scales", align_bytes=64)
-            packed[unit] = (codes, scales)
+            codes = mx_pool.tile([P, B * P], U32, name="codes_" + name, align_bytes=64)
+            scales = mx_pool.tile([P, B * P], U8, name="scales_" + name, align_bytes=64)
+            packed[(name, unit)] = (codes, scales)
             nc.vector.quantize_mx(
-                out=codes[:].rearrange("p s c -> p (s c)").bitcast(FP8X4),
-                scales=scales[:].rearrange("p s c -> p (s c)"),
-                in_=grouped[unit][:].rearrange("p s b r t -> p (s b r t)"),
+                out=codes[:].bitcast(FP8X4),
+                scales=scales[:],
+                in_=grouped[(name, unit)][:].rearrange("p b r t -> p (b r t)"),
             )
 
         def multiply(out, name, unit, b, first, count):
-            codes, scales = packed[unit]
+            codes, scales = packed[(name, unit)]
             nc.tensor.matmul_mx(
                 out=out,
-                lhsT=codes[:, SIDE[name], b * P : (b + 1) * P].bitcast(FP8X4),
-                lhsT_scale=scales[:, SIDE[name], b * P : (b + 1) * P],
+                lhsT=codes[:, b * P : (b + 1) * P].bitcast(FP8X4),
+                lhsT_scale=scales[:, b * P : (b + 1) * P],
                 rhs=w_codes[name][:, first * PACK : (first + count) * PACK].bitcast(FP8X4),
                 rhs_scale=w_plane[name][:, first : first + count],
                 start=True,
@@ -241,21 +240,22 @@ def tile_aftfull_pa_t_kernel(tc, k, v, Wk_words, Wk_scales, Wv_words, Wv_scales,
 
         for step in range(-3, UNITS + 1):
             regroup("k", step + 2)
-            regroup("v", step + 2)
+            regroup("v", step + 1)
+            max_of_pairs(step)
+            quantise("k", step + 1)
             project(k_banks, "k", step + 1, 1)
             copy_k_high(step + 1)
-            max_of_pairs(step)
-            weigh(step - 1, 0)
-            project(v_banks, "v", step, 0)
             max_of_batch(step)
             subtract_high(step)
+            weigh(step - 1, 0)
+            project(v_banks, "v", step, 0)
+            subtract_low(step)
+            project(k_banks, "k", step + 1, 0)
             weigh(step - 1, 1)
             store(weighted_dram, weighted_tiles, step - 1)
             project(v_banks, "v", step, 1)
-            subtract_low(step)
-            project(k_banks, "k", step + 1, 0)
             exponential(step)
             store(e_dram, e_tiles, step)
             transpose("k", step + 3)
-            transpose("v", step + 3)
-            quantise(step + 2)
+            transpose("v", step + 2)
+            quantise("v", step + 1)

@@ -251,11 +251,11 @@ def tile_aftfull_pa_t_kernel(tc, k, v, Wk_words, Wk_scales, Wv_words, Wv_scales,
             project(v_banks, "v", step, 0)
             subtract_low(step)
             project(k_banks, "k", step + 1, 0)
+            transpose("k", step + 3)
+            transpose("v", step + 2)
             weigh(step - 1, 1)
             store(weighted_dram, weighted_tiles, step - 1)
             project(v_banks, "v", step, 1)
             exponential(step)
             store(e_dram, e_tiles, step)
-            transpose("k", step + 3)
-            transpose("v", step + 2)
             quantise("v", step + 1)

@@ -20,7 +20,7 @@ UNITS = T // P
 PAIR = 2
 PAIRS = B // PAIR
 GROUP = 4
-LOAD_PIECES = (1, 2, 4, 4)
+LOADS = ((1, 1, 1, 1), (2, 2), (4,), (4,))
 SIDE = {"k": 0, "v": 1}
 IO_TAG = {"k": "k_e", "e": "k_e", "v": "v_w", "weighted": "v_w"}
 
@@ -74,10 +74,11 @@ def tile_aftfull_pa_t_kernel(tc, k, v, Wk_words, Wk_scales, Wv_words, Wv_scales,
             return 0 <= unit < UNITS
 
         def load(name, tile_of_group, first, count):
-            piece = (first % GROUP) // count
-            nc.sync.dma_start(out=tile_of_group[:, piece, :, :, :], in_=x_dram[name][:, :, first : first + count, :])
+            start = (first % GROUP) * B * DM
+            piece = tile_of_group[:, start : start + count * B * DM].rearrange("p (b j d) -> p b j d", b=B, j=count)
+            nc.sync.dma_start(out=piece, in_=x_dram[name][:, :, first : first + count, :])
             for i in range(count):
-                x_rows[(name, first + i)] = tile_of_group[:, piece, :, i, :]
+                x_rows[(name, first + i)] = piece[:, :, i, :]
 
         def load_weight(name):
             words, scale_rows = w_dram[name]
@@ -221,19 +222,22 @@ def tile_aftfull_pa_t_kernel(tc, k, v, Wk_words, Wk_scales, Wv_words, Wv_scales,
 
         identity = const.tile([P, P], F32, name="identity")
         make_identity(nc, identity[:])
-        weights_left = ["k", "v"]
-        for group, count in enumerate(LOAD_PIECES):
-            x_tiles = {}
-            for name in ("k", "v"):
-                x_tiles[name] = io_pool.tile(
-                    [P, GROUP // count, B, count, DM], BF16, name="x_" + name, tag=IO_TAG[name]
+        pieces = []
+        for group, counts in enumerate(LOADS):
+            first = group * GROUP
+            for count in counts:
+                pieces.append((first, "k", group, first, count))
+                pieces.append((first + 1, "v", group, first, count))
+                first += count
+        x_tiles = {}
+        for wanted, name, group, first, count in sorted(pieces):
+            if (name, group) not in x_tiles:
+                x_tiles[(name, group)] = io_pool.tile(
+                    [P, GROUP * B * DM], BF16, name="x_" + name, tag=IO_TAG[name]
                 )
-            for first in range(group * GROUP, (group + 1) * GROUP, count):
-                load("k", x_tiles["k"], first, count)
-                load("v", x_tiles["v"], first, count)
-                if weights_left:
-                    load_weight(weights_left[0])
-                    weights_left.remove(weights_left[0])
+            load(name, x_tiles[(name, group)], first, count)
+            if first == 0:
+                load_weight(name)
         warm = const.tile([P, 1], F32, name="warm")
         nc.vector.memset(warm[:], 0.0)
         nc.scalar.activation(out=warm[:], in_=warm[:], func=EXP)

@@ -20,7 +20,12 @@ UNITS = T // P
 PAIR = 2
 PAIRS = B // PAIR
 GROUP = 4
-LOADS = ((1, 1, 1, 1), (2, 2), (4,), (4,))
+LOADS = {
+    "k": ((1, 1, 1, 1), (2, 2), (4,), (4,)),
+    "v": ((1, 1, 2), (4,), (4,), (4,)),
+}
+STORES = (7, 4, 3, 2)
+FILL = 3
 SIDE = {"k": 0, "v": 1}
 IO_TAG = {"k": "k_e", "e": "k_e", "v": "v_w", "weighted": "v_w"}
 
@@ -39,7 +44,8 @@ def tile_aftfull_pa_t_kernel(tc, k, v, Wk_words, Wk_scales, Wv_words, Wv_scales,
 
     with ExitStack() as stack:
         const = stack.enter_context(tc.tile_pool(name="const", bufs=1))
-        io_pool = stack.enter_context(tc.tile_pool(name="io", bufs=UNITS // GROUP + 1))
+        first_pool = stack.enter_context(tc.tile_pool(name="first", bufs=1))
+        io_pool = stack.enter_context(tc.tile_pool(name="io", bufs=3))
         mx_pool = stack.enter_context(tc.tile_pool(name="mx", bufs=3))
         work_pool = stack.enter_context(tc.tile_pool(name="work", bufs=3))
         xt_pool = stack.enter_context(tc.psum_pool(name="xt", bufs=4))
@@ -61,14 +67,12 @@ def tile_aftfull_pa_t_kernel(tc, k, v, Wk_words, Wk_scales, Wv_words, Wv_scales,
         e_tiles = {}
         weighted_tiles = {}
 
-        stores = []
-        while sum(count for first, count in stores) < UNITS:
-            left = UNITS - sum(count for first, count in stores)
-            stores.append((UNITS - left, min(GROUP, max(1, left // 2))))
         store_of = {}
-        for first, count in stores:
+        first = 0
+        for count in STORES:
             for unit in range(first, first + count):
                 store_of[unit] = (first, count)
+            first += count
 
         def in_range(unit):
             return 0 <= unit < UNITS
@@ -110,7 +114,7 @@ def tile_aftfull_pa_t_kernel(tc, k, v, Wk_words, Wk_scales, Wv_words, Wv_scales,
             if not in_range(unit):
                 return
             grouped[(name, unit)] = mx_pool.tile([P, B, P, PACK], BF16, name="grouped_" + name, align_bytes=64)
-            for pair in range(PAIRS):
+            for pair in range(PAIRS) if unit < FILL else reversed(range(PAIRS)):
                 nc.scalar.copy(
                     out=grouped[(name, unit)][:, PAIR * pair : PAIR * (pair + 1), :, :].bitcast(F32),
                     in_=xt_banks[(name, unit, pair)][:].rearrange("p i w r -> p i r w"),
@@ -194,13 +198,20 @@ def tile_aftfull_pa_t_kernel(tc, k, v, Wk_words, Wk_scales, Wv_words, Wv_scales,
         def output_tile(tiles, name, unit):
             first, count = store_of[unit]
             if unit == first and first not in tiles:
-                tiles[first] = io_pool.tile([P, B, count, DH], F32, name=name, tag=IO_TAG[name])
+                pool = first_pool if first == 0 else io_pool
+                tiles[first] = pool.tile([P, B, count, DH], F32, name=name, tag=IO_TAG[name])
             return tiles[first][:, :, unit - first, :]
 
         def exponential(unit):
             if not in_range(unit):
                 return
-            nc.scalar.activation(out=output_tile(e_tiles, "e", unit), in_=diff[unit][:], func=EXP)
+            items = B if unit < UNITS - 1 else PAIR
+            for b in range(0, B, items):
+                nc.scalar.activation(
+                    out=output_tile(e_tiles, "e", unit)[:, b : b + items, :],
+                    in_=diff[unit][:, b : b + items, :],
+                    func=EXP,
+                )
 
         def weigh(unit, pair):
             if not in_range(unit):
@@ -223,26 +234,34 @@ def tile_aftfull_pa_t_kernel(tc, k, v, Wk_words, Wk_scales, Wv_words, Wv_scales,
         identity = const.tile([P, P], F32, name="identity")
         make_identity(nc, identity[:])
         pieces = []
-        for group, counts in enumerate(LOADS):
-            first = group * GROUP
-            for count in counts:
-                pieces.append((first, "k", group, first, count))
-                pieces.append((first + 1, "v", group, first, count))
-                first += count
+        for name in sorted(LOADS):
+            for group, counts in enumerate(LOADS[name]):
+                first = group * GROUP
+                for count in counts:
+                    pieces.append((first + SIDE[name], name, group, first, count))
+                    first += count
         x_tiles = {}
-        for wanted, name, group, first, count in sorted(pieces):
-            if (name, group) not in x_tiles:
-                x_tiles[(name, group)] = io_pool.tile(
-                    [P, GROUP * B * DM], BF16, name="x_" + name, tag=IO_TAG[name]
-                )
-            load(name, x_tiles[(name, group)], first, count)
-            if first == 0:
-                load_weight(name)
+
+        def load_groups(groups):
+            for wanted, name, group, first, count in sorted(pieces):
+                if group not in groups:
+                    continue
+                if (name, group) not in x_tiles:
+                    x_tiles[(name, group)] = io_pool.tile(
+                        [P, GROUP * B * DM], BF16, name="x_" + name, tag=IO_TAG[name]
+                    )
+                load(name, x_tiles[(name, group)], first, count)
+                if first == 0:
+                    load_weight(name)
+
+        load_groups(range(UNITS // GROUP - 1))
         warm = const.tile([P, 1], F32, name="warm")
         nc.vector.memset(warm[:], 0.0)
         nc.scalar.activation(out=warm[:], in_=warm[:], func=EXP)
 
         for step in range(-3, UNITS + 1):
+            if step == 2:
+                load_groups([UNITS // GROUP - 1])
             regroup("k", step + 2)
             regroup("v", step + 1)
             max_of_pairs(step)
@@ -251,9 +270,12 @@ def tile_aftfull_pa_t_kernel(tc, k, v, Wk_words, Wk_scales, Wv_words, Wv_scales,
             copy_k_high(step + 1)
             max_of_batch(step)
             subtract_high(step)
+            if step == UNITS - 1:
+                subtract_low(step)
             weigh(step - 1, 0)
             project(v_banks, "v", step, 0)
-            subtract_low(step)
+            if step < UNITS - 1:
+                subtract_low(step)
             project(k_banks, "k", step + 1, 0)
             transpose("k", step + 3)
             transpose("v", step + 2)

@@ -19,15 +19,19 @@ WORDS = DM // 2
 UNITS = T // P
 PAIR = 2
 PAIRS = B // PAIR
-GROUP = 4
 LOADS = {
     "k": ((1, 1, 1, 1), (2, 2), (4,), (4,)),
-    "v": ((1, 1, 2), (4,), (4,), (4,)),
+    "v": ((1, 1, 2), (4,), (8,)),
 }
-STORES = (7, 4, 3, 2)
+STORES = {"e": (7, 4, 3, 2), "weighted": (8, 4, 2, 2)}
 FILL = 3
 SIDE = {"k": 0, "v": 1}
-IO_TAG = {"k": "k_e", "e": "k_e", "v": "v_w", "weighted": "v_w"}
+PLACES = {
+    "k": ("k_e", "k_e", "k_e", "k_e"),
+    "e": ("e_first", "k_e", "k_e", "k_e"),
+    "v": ("v_w", "v_w", "v_late"),
+    "weighted": ("w_first", "v_w", "v_w", "v_late"),
+}
 
 FLOPS = 2 * 2 * B * T * DM * DH
 
@@ -44,10 +48,15 @@ def tile_aftfull_pa_t_kernel(tc, k, v, Wk_words, Wk_scales, Wv_words, Wv_scales,
 
     with ExitStack() as stack:
         const = stack.enter_context(tc.tile_pool(name="const", bufs=1))
-        first_pool = stack.enter_context(tc.tile_pool(name="first", bufs=1))
-        io_pool = stack.enter_context(tc.tile_pool(name="io", bufs=3))
-        mx_pool = stack.enter_context(tc.tile_pool(name="mx", bufs=3))
+        single_pool = stack.enter_context(tc.tile_pool(name="single", bufs=1))
+        place_pools = {
+            "k_e": stack.enter_context(tc.tile_pool(name="k_e", bufs=3)),
+            "v_w": stack.enter_context(tc.tile_pool(name="v_w", bufs=2)),
+        }
+        grouped_pool = stack.enter_context(tc.tile_pool(name="grouped", bufs=3))
+        mx_pool = stack.enter_context(tc.tile_pool(name="mx", bufs=2))
         work_pool = stack.enter_context(tc.tile_pool(name="work", bufs=3))
+        top_pool = stack.enter_context(tc.tile_pool(name="top", bufs=2))
         xt_pool = stack.enter_context(tc.psum_pool(name="xt", bufs=4))
         acc_pool = stack.enter_context(tc.psum_pool(name="acc", bufs=1))
         stack.enter_context(tc.manual_schedule())
@@ -68,18 +77,23 @@ def tile_aftfull_pa_t_kernel(tc, k, v, Wk_words, Wk_scales, Wv_words, Wv_scales,
         weighted_tiles = {}
 
         store_of = {}
-        first = 0
-        for count in STORES:
-            for unit in range(first, first + count):
-                store_of[unit] = (first, count)
-            first += count
+        for name in STORES:
+            first = 0
+            for index, count in enumerate(STORES[name]):
+                for unit in range(first, first + count):
+                    store_of[(name, unit)] = (index, first, count)
+                first += count
 
         def in_range(unit):
             return 0 <= unit < UNITS
 
-        def load(name, tile_of_group, first, count):
-            start = (first % GROUP) * B * DM
-            piece = tile_of_group[:, start : start + count * B * DM].rearrange("p (b j d) -> p b j d", b=B, j=count)
+        def new_tile(name, index, shape, dtype):
+            place = PLACES[name][index]
+            pool = place_pools.get(place, single_pool)
+            return pool.tile(shape, dtype, name="%s_tile" % name, tag=place)
+
+        def load(name, tile, start, first, count):
+            piece = tile[:, start * B * DM : (start + count) * B * DM].rearrange("p (b j d) -> p b j d", b=B, j=count)
             nc.sync.dma_start(out=piece, in_=x_dram[name][:, :, first : first + count, :])
             for i in range(count):
                 x_rows[(name, first + i)] = piece[:, :, i, :]
@@ -113,7 +127,7 @@ def tile_aftfull_pa_t_kernel(tc, k, v, Wk_words, Wk_scales, Wv_words, Wv_scales,
         def regroup(name, unit):
             if not in_range(unit):
                 return
-            grouped[(name, unit)] = mx_pool.tile([P, B, P, PACK], BF16, name="grouped_" + name, align_bytes=64)
+            grouped[(name, unit)] = grouped_pool.tile([P, B, P, PACK], BF16, name="grouped_" + name, align_bytes=64)
             for pair in range(PAIRS) if unit < FILL else reversed(range(PAIRS)):
                 nc.scalar.copy(
                     out=grouped[(name, unit)][:, PAIR * pair : PAIR * (pair + 1), :, :].bitcast(F32),
@@ -161,7 +175,7 @@ def tile_aftfull_pa_t_kernel(tc, k, v, Wk_words, Wk_scales, Wv_words, Wv_scales,
         def max_of_pairs(unit):
             if not in_range(unit):
                 return
-            pair_top[unit] = work_pool.tile([P, PAIR, DH], F32, name="pair_top")
+            pair_top[unit] = top_pool.tile([P, PAIR, DH], F32, name="pair_top")
             nc.vector.tensor_tensor(
                 out=pair_top[unit][:], in0=k_banks[(unit, 0)][:], in1=k_high[unit][:], op=ALU.max
             )
@@ -169,7 +183,7 @@ def tile_aftfull_pa_t_kernel(tc, k, v, Wk_words, Wk_scales, Wv_words, Wv_scales,
         def max_of_batch(unit):
             if not in_range(unit):
                 return
-            top[unit] = work_pool.tile([P, DH], F32, name="top")
+            top[unit] = top_pool.tile([P, DH], F32, name="top")
             nc.vector.tensor_tensor(
                 out=top[unit][:], in0=pair_top[unit][:, 0, :], in1=pair_top[unit][:, 1, :], op=ALU.max
             )
@@ -196,11 +210,10 @@ def tile_aftfull_pa_t_kernel(tc, k, v, Wk_words, Wk_scales, Wv_words, Wv_scales,
             )
 
         def output_tile(tiles, name, unit):
-            first, count = store_of[unit]
-            if unit == first and first not in tiles:
-                pool = first_pool if first == 0 else io_pool
-                tiles[first] = pool.tile([P, B, count, DH], F32, name=name, tag=IO_TAG[name])
-            return tiles[first][:, :, unit - first, :]
+            index, first, count = store_of[(name, unit)]
+            if index not in tiles:
+                tiles[index] = new_tile(name, index, [P, B, count, DH], F32)
+            return tiles[index][:, :, unit - first, :]
 
         def exponential(unit):
             if not in_range(unit):
@@ -224,44 +237,44 @@ def tile_aftfull_pa_t_kernel(tc, k, v, Wk_words, Wk_scales, Wv_words, Wv_scales,
                 op=ALU.mult,
             )
 
-        def store(dram, tiles, unit):
+        def store(dram, tiles, name, unit):
             if not in_range(unit):
                 return
-            first, count = store_of[unit]
+            index, first, count = store_of[(name, unit)]
             if unit == first + count - 1:
-                nc.sync.dma_start(out=dram[:, :, first : first + count, :], in_=tiles[first][:])
+                nc.sync.dma_start(out=dram[:, :, first : first + count, :], in_=tiles[index][:])
 
         identity = const.tile([P, P], F32, name="identity")
         make_identity(nc, identity[:])
         pieces = []
         for name in sorted(LOADS):
-            for group, counts in enumerate(LOADS[name]):
-                first = group * GROUP
+            first = 0
+            for index, counts in enumerate(LOADS[name]):
+                start = 0
                 for count in counts:
-                    pieces.append((first + SIDE[name], name, group, first, count))
+                    pieces.append((first + SIDE[name], name, index, start, first, count))
+                    start += count
                     first += count
         x_tiles = {}
 
-        def load_groups(groups):
-            for wanted, name, group, first, count in sorted(pieces):
-                if group not in groups:
+        def load_pieces(late):
+            for wanted, name, index, start, first, count in sorted(pieces):
+                if late != (PLACES[name][index] in PLACES[name][: index] and index == len(LOADS[name]) - 1):
                     continue
-                if (name, group) not in x_tiles:
-                    x_tiles[(name, group)] = io_pool.tile(
-                        [P, GROUP * B * DM], BF16, name="x_" + name, tag=IO_TAG[name]
-                    )
-                load(name, x_tiles[(name, group)], first, count)
+                if (name, index) not in x_tiles:
+                    x_tiles[(name, index)] = new_tile(name, index, [P, sum(LOADS[name][index]) * B * DM], BF16)
+                load(name, x_tiles[(name, index)], start, first, count)
                 if first == 0:
                     load_weight(name)
 
-        load_groups(range(UNITS // GROUP - 1))
+        load_pieces(False)
         warm = const.tile([P, 1], F32, name="warm")
         nc.vector.memset(warm[:], 0.0)
         nc.scalar.activation(out=warm[:], in_=warm[:], func=EXP)
 
         for step in range(-3, UNITS + 1):
             if step == 2:
-                load_groups([UNITS // GROUP - 1])
+                load_pieces(True)
             regroup("k", step + 2)
             regroup("v", step + 1)
             max_of_pairs(step)
@@ -280,8 +293,8 @@ def tile_aftfull_pa_t_kernel(tc, k, v, Wk_words, Wk_scales, Wv_words, Wv_scales,
             transpose("k", step + 3)
             transpose("v", step + 2)
             weigh(step - 1, 1)
-            store(weighted_dram, weighted_tiles, step - 1)
+            store(weighted_dram, weighted_tiles, "weighted", step - 1)
             project(v_banks, "v", step, 1)
             exponential(step)
-            store(e_dram, e_tiles, step)
+            store(e_dram, e_tiles, "e", step)
             quantise("v", step + 1)

@@ -20,7 +20,7 @@ UNITS = T // P
 PAIR = 2
 PAIRS = B // PAIR
 LOADS = {
-    "k": ((1, 1, 1, 1), (2, 2), (4,), (4,)),
+    "k": ((1, 1, 2), (2, 2), (4,), (4,)),
     "v": ((1, 1, 2), (4,), (8,)),
 }
 STORES = {"e": (7, 4, 3, 2), "weighted": (8, 4, 2, 2)}
@@ -264,7 +264,7 @@ def tile_aftfull_pa_t_kernel(tc, k, v, Wk_words, Wk_scales, Wv_words, Wv_scales,
                 if (name, index) not in x_tiles:
                     x_tiles[(name, index)] = new_tile(name, index, [P, sum(LOADS[name][index]) * B * DM], BF16)
                 load(name, x_tiles[(name, index)], start, first, count)
-                if first == 0:
+                if first == SIDE[name]:
                     load_weight(name)
 
         load_pieces(False)

@@ -20,7 +20,7 @@ UNITS = T // P
 PAIR = 2
 PAIRS = B // PAIR
 LOADS = {
-    "k": ((1, 1, 2), (2, 2), (4,), (4,)),
+    "k": ((2, 2), (2, 2), (4,), (4,)),
     "v": ((1, 1, 2), (4,), (8,)),
 }
 STORES = {"e": (7, 4, 3, 2), "weighted": (8, 4, 2, 2)}

from contextlib import ExitStack

import concourse.mybir as mybir
from concourse.masks import make_identity

F32 = mybir.dt.float32
BF16 = mybir.dt.bfloat16
I32 = mybir.dt.int32
U32 = mybir.dt.uint32
U8 = mybir.dt.uint8
FP8X4 = mybir.dt.float8_e4m3fn_x4
ALU = mybir.AluOpType
EXP = mybir.ActivationFunctionType.Exp

B, T, DM, DH = 4, 2048, 512, 256
P = 128
PACK = 4
WORDS = DM // 2
UNITS = T // P
PAIR = 2
PAIRS = B // PAIR
LOADS = {
    "k": ((2, 2), (2, 2), (4,), (4,)),
    "v": ((1, 1, 2), (4,), (8,)),
}
STORES = {"e": (7, 4, 3, 2), "weighted": (8, 4, 2, 2)}
FILL = 3
SIDE = {"k": 0, "v": 1}
PLACES = {
    "k": ("k_e", "k_e", "k_e", "k_e"),
    "e": ("e_first", "k_e", "k_e", "k_e"),
    "v": ("v_w", "v_w", "v_late"),
    "weighted": ("w_first", "v_w", "v_w", "v_late"),
}

FLOPS = 2 * 2 * B * T * DM * DH


def tile_aftfull_pa_t_kernel(tc, k, v, Wk_words, Wk_scales, Wv_words, Wv_scales, out_0, out_1):
    nc = tc.nc
    x_dram = {
        "k": k.rearrange("b (p j) d -> p b j d", j=UNITS),
        "v": v.rearrange("b (p j) d -> p b j d", j=UNITS),
    }
    w_dram = {"k": (Wk_words, Wk_scales), "v": (Wv_words, Wv_scales)}
    weighted_dram = out_0.rearrange("b (p j) c -> p b j c", j=UNITS)
    e_dram = out_1.rearrange("b (p j) c -> p b j c", j=UNITS)

    with ExitStack() as stack:
        const = stack.enter_context(tc.tile_pool(name="const", bufs=1))
        single_pool = stack.enter_context(tc.tile_pool(name="single", bufs=1))
        place_pools = {
            "k_e": stack.enter_context(tc.tile_pool(name="k_e", bufs=3)),
            "v_w": stack.enter_context(tc.tile_pool(name="v_w", bufs=2)),
        }
        grouped_pool = stack.enter_context(tc.tile_pool(name="grouped", bufs=3))
        mx_pool = stack.enter_context(tc.tile_pool(name="mx", bufs=2))
        work_pool = stack.enter_context(tc.tile_pool(name="work", bufs=3))
        top_pool = stack.enter_context(tc.tile_pool(name="top", bufs=2))
        xt_pool = stack.enter_context(tc.psum_pool(name="xt", bufs=4))
        acc_pool = stack.enter_context(tc.psum_pool(name="acc", bufs=1))
        stack.enter_context(tc.manual_schedule())

        x_rows = {}
        xt_banks = {}
        grouped = {}
        packed = {}
        w_codes = {}
        w_plane = {}
        k_banks = {}
        v_banks = {}
        k_high = {}
        pair_top = {}
        top = {}
        diff = {}
        e_tiles = {}
        weighted_tiles = {}

        store_of = {}
        for name in STORES:
            first = 0
            for index, count in enumerate(STORES[name]):
                for unit in range(first, first + count):
                    store_of[(name, unit)] = (index, first, count)
                first += count

        def in_range(unit):
            return 0 <= unit < UNITS

        def new_tile(name, index, shape, dtype):
            place = PLACES[name][index]
            pool = place_pools.get(place, single_pool)
            return pool.tile(shape, dtype, name="%s_tile" % name, tag=place)

        def load(name, tile, start, first, count):
            piece = tile[:, start * B * DM : (start + count) * B * DM].rearrange("p (b j d) -> p b j d", b=B, j=count)
            nc.sync.dma_start(out=piece, in_=x_dram[name][:, :, first : first + count, :])
            for i in range(count):
                x_rows[(name, first + i)] = piece[:, :, i, :]

        def load_weight(name):
            words, scale_rows = w_dram[name]
            w_codes[name] = const.tile([P, DH * PACK], U8, name="w_codes_" + name, align_bytes=64)
            w_plane[name] = const.tile([P, DH], U8, name="w_plane_" + name, align_bytes=64)
            nc.vector.memset(w_plane[name][:].bitcast(I32), 0)
            nc.sync.dma_start(
                out=w_codes[name][:].bitcast(I32),
                in_=words[0].rearrange("p n t -> p (n t)").bitcast(I32),
            )
            for quadrant in range(4):
                nc.sync.dma_start(
                    out=w_plane[name][32 * quadrant : 32 * quadrant + 4, :].bitcast(I32),
                    in_=scale_rows[0, 4 * quadrant : 4 * quadrant + 4, :].bitcast(I32),
                )

        def transpose(name, unit):
            if not in_range(unit):
                return
            for pair in range(PAIRS):
                bank = xt_pool.tile([P, PAIR, 2, P], F32, name="xt")
                xt_banks[(name, unit, pair)] = bank
                for i in range(PAIR):
                    row_words = x_rows[(name, unit)][:, PAIR * pair + i, :].bitcast(F32)
                    for w in range(2):
                        nc.tensor.transpose(bank[:, i, w, :], row_words[:, w:WORDS:2], identity[:])

        def regroup(name, unit):
            if not in_range(unit):
                return
            grouped[(name, unit)] = grouped_pool.tile([P, B, P, PACK], BF16, name="grouped_" + name, align_bytes=64)
            for pair in range(PAIRS) if unit < FILL else reversed(range(PAIRS)):
                nc.scalar.copy(
                    out=grouped[(name, unit)][:, PAIR * pair : PAIR * (pair + 1), :, :].bitcast(F32),
                    in_=xt_banks[(name, unit, pair)][:].rearrange("p i w r -> p i r w"),
                )

        def quantise(name, unit):
            if not in_range(unit):
                return
            codes = mx_pool.tile([P, B * P], U32, name="codes_" + name, align_bytes=64)
            scales = mx_pool.tile([P, B * P], U8, name="scales_" + name, align_bytes=64)
            packed[(name, unit)] = (codes, scales)
            nc.vector.quantize_mx(
                out=codes[:].bitcast(FP8X4),
                scales=scales[:],
                in_=grouped[(name, unit)][:].rearrange("p b r t -> p (b r t)"),
            )

        def multiply(out, name, unit, b, first, count):
            codes, scales = packed[(name, unit)]
            nc.tensor.matmul_mx(
                out=out,
                lhsT=codes[:, b * P : (b + 1) * P].bitcast(FP8X4),
                lhsT_scale=scales[:, b * P : (b + 1) * P],
                rhs=w_codes[name][:, first * PACK : (first + count) * PACK].bitcast(FP8X4),
                rhs_scale=w_plane[name][:, first : first + count],
                start=True,
                stop=True,
            )

        def project(banks, name, unit, pair):
            if not in_range(unit):
                return
            bank = acc_pool.tile([P, PAIR, DH], F32, name="%s_bank%d" % (name, pair))
            banks[(unit, pair)] = bank
            for i in range(PAIR):
                multiply(bank[:, i, :], name, unit, PAIR * pair + i, 0, DH)

        def copy_k_high(unit):
            if not in_range(unit):
                return
            k_high[unit] = work_pool.tile([P, PAIR, DH], F32, name="k_high")
            nc.scalar.copy(out=k_high[unit][:], in_=k_banks[(unit, 1)][:])

        def max_of_pairs(unit):
            if not in_range(unit):
                return
            pair_top[unit] = top_pool.tile([P, PAIR, DH], F32, name="pair_top")
            nc.vector.tensor_tensor(
                out=pair_top[unit][:], in0=k_banks[(unit, 0)][:], in1=k_high[unit][:], op=ALU.max
            )

        def max_of_batch(unit):
            if not in_range(unit):
                return
            top[unit] = top_pool.tile([P, DH], F32, name="top")
            nc.vector.tensor_tensor(
                out=top[unit][:], in0=pair_top[unit][:, 0, :], in1=pair_top[unit][:, 1, :], op=ALU.max
            )
            diff[unit] = work_pool.tile([P, B, DH], F32, name="diff")

        def subtract_high(unit):
            if not in_range(unit):
                return
            nc.gpsimd.tensor_tensor(
                out=diff[unit][:, PAIR:B, :],
                in0=k_high[unit][:],
                in1=top[unit][:].unsqueeze(1).to_broadcast([P, PAIR, DH]),
                op=ALU.subtract,
            )

        def subtract_low(unit):
            if not in_range(unit):
                return
            nc.vector.tensor_tensor(
                out=diff[unit][:, 0:PAIR, :],
                in0=k_banks[(unit, 0)][:],
                in1=top[unit][:].unsqueeze(1).to_broadcast([P, PAIR, DH]),
                op=ALU.subtract,
            )

        def output_tile(tiles, name, unit):
            index, first, count = store_of[(name, unit)]
            if index not in tiles:
                tiles[index] = new_tile(name, index, [P, B, count, DH], F32)
            return tiles[index][:, :, unit - first, :]

        def exponential(unit):
            if not in_range(unit):
                return
            items = B if unit < UNITS - 1 else PAIR
            for b in range(0, B, items):
                nc.scalar.activation(
                    out=output_tile(e_tiles, "e", unit)[:, b : b + items, :],
                    in_=diff[unit][:, b : b + items, :],
                    func=EXP,
                )

        def weigh(unit, pair):
            if not in_range(unit):
                return
            items = slice(PAIR * pair, PAIR * (pair + 1))
            nc.vector.tensor_tensor(
                out=output_tile(weighted_tiles, "weighted", unit)[:, items, :],
                in0=v_banks[(unit, pair)][:],
                in1=output_tile(e_tiles, "e", unit)[:, items, :],
                op=ALU.mult,
            )

        def store(dram, tiles, name, unit):
            if not in_range(unit):
                return
            index, first, count = store_of[(name, unit)]
            if unit == first + count - 1:
                nc.sync.dma_start(out=dram[:, :, first : first + count, :], in_=tiles[index][:])

        identity = const.tile([P, P], F32, name="identity")
        make_identity(nc, identity[:])
        pieces = []
        for name in sorted(LOADS):
            first = 0
            for index, counts in enumerate(LOADS[name]):
                start = 0
                for count in counts:
                    pieces.append((first + SIDE[name], name, index, start, first, count))
                    start += count
                    first += count
        x_tiles = {}

        def load_pieces(late):
            for wanted, name, index, start, first, count in sorted(pieces):
                if late != (PLACES[name][index] in PLACES[name][: index] and index == len(LOADS[name]) - 1):
                    continue
                if (name, index) not in x_tiles:
                    x_tiles[(name, index)] = new_tile(name, index, [P, sum(LOADS[name][index]) * B * DM], BF16)
                load(name, x_tiles[(name, index)], start, first, count)
                if first == SIDE[name]:
                    load_weight(name)

        load_pieces(False)
        warm = const.tile([P, 1], F32, name="warm")
        nc.vector.memset(warm[:], 0.0)
        nc.scalar.activation(out=warm[:], in_=warm[:], func=EXP)

        for step in range(-3, UNITS + 1):
            if step == 2:
                load_pieces(True)
            regroup("k", step + 2)
            regroup("v", step + 1)
            max_of_pairs(step)
            quantise("k", step + 1)
            project(k_banks, "k", step + 1, 1)
            copy_k_high(step + 1)
            max_of_batch(step)
            subtract_high(step)
            if step == UNITS - 1:
                subtract_low(step)
            weigh(step - 1, 0)
            project(v_banks, "v", step, 0)
            if step < UNITS - 1:
                subtract_low(step)
            project(k_banks, "k", step + 1, 0)
            transpose("k", step + 3)
            transpose("v", step + 2)
            weigh(step - 1, 1)
            store(weighted_dram, weighted_tiles, "weighted", step - 1)
            project(v_banks, "v", step, 1)
            exponential(step)
            store(e_dram, e_tiles, "e", step)
            quantise("v", step + 1)
